import numpy as np
import ml_dtypes


def mxq(x, axis, fmt="e4m3"):
    dtype, down = {"e4m3": (ml_dtypes.float8_e4m3fn, 7), "e5m2": (ml_dtypes.float8_e5m2, 14)}[fmt]
    v = np.moveaxis(np.asarray(x, np.float32).astype(ml_dtypes.bfloat16).astype(np.float64), axis, -1)
    blocks = v.reshape(v.shape[:-1] + (-1, 32))
    amax = np.abs(blocks).max(-1, keepdims=True)
    byte = np.maximum(np.where(amax > 0, np.frexp(amax)[1] - 1 + 127, 0) - down, 1)
    scale = np.exp2(byte - 127.0)
    codes = (blocks / scale).astype(np.float32).astype(dtype).astype(np.float64)
    return np.moveaxis((codes * scale).reshape(v.shape), -1, axis)


WIDE = False


def mx_kscale(k):
    if not WIDE:
        return np.ones(k)
    levels = np.array([10, -10, 5, -5, 0])
    a = np.random.permutation(np.resize(levels, k // 512 * 4)).reshape(k // 512, 4)
    idx = np.arange(k)
    return np.exp2(a[idx // 512, idx % 128 // 32])


BF16 = ml_dtypes.bfloat16


def bf(x):
    return np.asarray(x, np.float32).astype(BF16)


def f64(x):
    return np.asarray(x).astype(np.float64)


E2M1 = np.array([0.0, 0.5, 1.0, 1.5, 2.0, 3.0, 4.0, 6.0, -0.0, -0.5, -1.0, -1.5, -2.0, -3.0, -4.0, -6.0])


def pack_weight(w, fmt):
    k, n = w.shape
    w = f64(bf(w)).reshape(k // 32, 32, n)
    amax = np.abs(w).max(1)
    if fmt == "e4m3":
        byte = np.frexp(amax)[1] - 1 + 127 - 7
    else:
        mant, ex = np.frexp(amax / 6.0)
        byte = np.where(mant > 0.5, ex, ex - 1) + 127
    byte = np.clip(np.where(amax > 0, byte, 1), 1, 254)
    scaled = (w * np.exp2(127.0 - byte)[:, None, :]).reshape(k, n).astype(np.float32)
    by_word = np.ascontiguousarray(scaled.reshape(k // 512, 128, 4, n).transpose(0, 1, 3, 2))
    if fmt == "e4m3":
        words = by_word.astype(ml_dtypes.float8_e4m3fn).view(np.uint8)
    else:
        c = by_word.astype(ml_dtypes.float4_e2m1fn).view(np.uint8) & 0xF
        words = c[..., 0::2] | (c[..., 1::2] << 4)
    return np.ascontiguousarray(words), np.ascontiguousarray(byte.astype(np.uint8).reshape(k // 512, 16, n))


def unpack_weight(words, scales, fmt):
    g, p, n, _ = words.shape
    if fmt == "e4m3":
        vals = np.ascontiguousarray(words).view(ml_dtypes.float8_e4m3fn).astype(np.float64)
    else:
        nib = np.empty((g, p, n, 4), np.uint8)
        nib[..., 0::2] = words & 0xF
        nib[..., 1::2] = words >> 4
        vals = E2M1[nib]
    vals = vals * np.repeat(np.exp2(scales.astype(np.float64) - 127.0), 8, axis=1)[..., None]
    return vals.transpose(0, 1, 3, 2).reshape(g * 512, n)

def pack4(w):
    words, scales = pack_weight(w, "e2m1")
    return words.reshape(words.shape[0], 128, -1), scales


def unpack4(words, scales):
    return unpack_weight(words.reshape(words.shape[0], 128, -1, 2), scales, "e2m1")


B, N, C0, C1, C2, O0, O1, O2 = 16, 16, 512, 512, 512, 512, 2048, 512
G = C1 + C2
K = 2 * G


def sigmoid(v):
    return 1.0 / (1.0 + np.exp(-v))


def setup_inputs():
    s = mx_kscale(G)
    ss = np.concatenate([s, s])
    x1 = bf(np.random.random((B, N, C1)) * s[:C1])
    x2 = bf(np.random.random((B, N, N, C2)) * s[C1:])
    W2_words, W2_scales = pack4(np.random.standard_normal((K, O2)) * 2.0 / np.sqrt(K) / ss[:, None])
    b2 = bf(np.random.standard_normal(O2) * 0.3)
    return {"x1": x1,
            "x2": x2,
            "W2_words": W2_words,
            "W2_scales": W2_scales,
            "b2": b2}


def reference(x1, x2, W2_words, W2_scales, b2):
    x1, x2 = f64(x1), f64(x2)
    e1 = np.broadcast_to(x1[:, :, None, :], (B, N, N, C1))
    g = np.concatenate([e1, x2], axis=-1)
    f2 = np.concatenate([g, np.swapaxes(g, 1, 2)], axis=-1)
    return sigmoid((mxq(f2, 3, "e4m3") @ unpack4(W2_words, W2_scales)) + f64(b2))

@@ -1,0 +1,184 @@
+from contextlib import ExitStack
+
+import concourse.mybir as mybir
+from concourse.masks import make_identity
+
+F32 = mybir.dt.float32
+BF16 = mybir.dt.bfloat16
+I32 = mybir.dt.int32
+U32 = mybir.dt.uint32
+U8 = mybir.dt.uint8
+FP8X4 = mybir.dt.float8_e4m3fn_x4
+FP4X4 = mybir.dt.float4_e2m1fn_x4
+
+P = 128
+SCENES = 16
+OBJECTS = 16
+CHANNELS = 512
+HALVES = 2
+HALF_SCENES = SCENES // HALVES
+WORDS = CHANNELS // 2
+CHUNK = 4
+BANK_SLICES = 2
+
+W_X1_I = 0
+W_X2_IJ = 1
+W_X1_J = 2
+W_X2_JI = 3
+
+FLOPS = 2 * SCENES * OBJECTS * OBJECTS * 4 * CHANNELS * CHANNELS
+
+
+def tile_differentiablelogicmachine_pa_kernel(tc, x1, x2, W2_words, W2_scales, b2, out):
+    nc = tc.nc
+    add = mybir.AluOpType.add
+    sigmoid = mybir.ActivationFunctionType.Sigmoid
+
+    with ExitStack() as ctx:
+        ctx.enter_context(tc.manual_schedule())
+        keep = ctx.enter_context(tc.tile_pool(name="keep", bufs=1))
+        stage = ctx.enter_context(tc.tile_pool(name="stage", bufs=4))
+        psum_t = ctx.enter_context(tc.psum_pool(name="psum_t", bufs=4))
+        psum_acc = ctx.enter_context(tc.psum_pool(name="psum_acc", bufs=4))
+
+        x1_raw = keep.tile([P, HALVES, CHANNELS], BF16)
+        x2_raw = keep.tile([P, HALVES, OBJECTS, CHANNELS], BF16)
+        w_words = keep.tile([P, 4, 2 * CHANNELS], U8, align_bytes=64)
+        w_scales = keep.tile([P, 4, CHANNELS], U8, align_bytes=64)
+        x1_codes = keep.tile([P, HALVES, P], U32, align_bytes=64)
+        x1_scales = keep.tile([P, HALVES, P], U8, align_bytes=64)
+        ji_codes = keep.tile([P, HALVES, OBJECTS, P], U32, align_bytes=64)
+        ji_scales = keep.tile([P, HALVES, OBJECTS, P], U8, align_bytes=64)
+        ij_codes = keep.tile([P, HALVES, OBJECTS, P], U32, align_bytes=64)
+        ij_scales = keep.tile([P, HALVES, OBJECTS, P], U8, align_bytes=64)
+        i_codes = keep.tile([P, HALVES, OBJECTS, P], U32, align_bytes=64)
+        i_scales = keep.tile([P, HALVES, OBJECTS, P], U8, align_bytes=64)
+        identity = keep.tile([P, P], F32)
+        ones = keep.tile([P, P], BF16)
+        bias_row = keep.tile([P, CHANNELS], BF16)
+        bias_all = keep.tile([P, CHANNELS], F32)
+        j_term = keep.tile([P, HALVES, CHANNELS], F32)
+        warm_in = keep.tile([P, 1], F32)
+        warm_out = keep.tile([P, 1], F32)
+
+        nc.vector.memset(w_scales[:].bitcast(I32), 0)
+        nc.vector.memset(x1_scales[:].bitcast(I32), 0)
+        nc.vector.memset(ji_scales[:].bitcast(I32), 0)
+        nc.vector.memset(bias_row[:], 0.0)
+        nc.vector.memset(ones[:], 1.0)
+        nc.vector.memset(warm_in[:], 0.0)
+        nc.scalar.activation(out=warm_out[:], in_=warm_in[:], func=sigmoid)
+        make_identity(nc, identity[:])
+
+        for h in range(HALVES):
+            scenes = slice(h * HALF_SCENES, (h + 1) * HALF_SCENES)
+            nc.sync.dma_start(out=x1_raw[:, h, :], in_=x1[scenes].rearrange("b i k -> i b k"))
+        for r in range(4):
+            nc.sync.dma_start(
+                out=w_scales[r:P:32, :, :].bitcast(I32),
+                in_=W2_scales[:, r:16:4, :].bitcast(I32).rearrange("g q n -> q g n"),
+            )
+        nc.sync.dma_start(out=bias_row[0:1, :], in_=b2.rearrange("(o c) -> o c", o=1))
+
+        def load_x2_chunk(h, c):
+            scenes = slice(h * HALF_SCENES, (h + 1) * HALF_SCENES)
+            slices = slice(c * CHUNK, (c + 1) * CHUNK)
+            nc.sync.dma_start(
+                out=x2_raw[:, h, slices, :].rearrange("p q k -> p (q k)"),
+                in_=x2[scenes, :, slices, :].rearrange("b p q k -> p b (q k)"),
+            )
+
+        for c in range(OBJECTS // CHUNK):
+            load_x2_chunk(0, c)
+        nc.sync.dma_start(out=w_words[:].bitcast(I32), in_=W2_words.bitcast(I32).rearrange("g p n -> p g n"))
+        for c in range(OBJECTS // CHUNK):
+            load_x2_chunk(1, c)
+
+        def transpose_bank(rows_of_slice, grouped_words):
+            bank = psum_t.tile([P, 2, BANK_SLICES, P], F32)
+            for s in range(BANK_SLICES):
+                for u in range(2):
+                    nc.tensor.transpose(bank[:, u, s, :], rows_of_slice[s].bitcast(F32)[:, u:WORDS:2], identity[:])
+            nc.scalar.copy(out=grouped_words, in_=bank[:].rearrange("p u s c -> p s c u"))
+
+        x1_grouped = keep.tile([P, HALVES * P * 4], BF16, align_bytes=64)
+        transpose_bank(
+            [x1_raw[:, h, :] for h in range(HALVES)],
+            x1_grouped[:].bitcast(F32).rearrange("p (s c u) -> p s c u", s=BANK_SLICES, u=2),
+        )
+        nc.vector.quantize_mx(
+            out=x1_codes[:].rearrange("p h c -> p (h c)").bitcast(FP8X4),
+            scales=x1_scales[:].rearrange("p h c -> p (h c)"),
+            in_=x1_grouped[:],
+        )
+        for h in range(HALVES):
+            nc.vector.tensor_copy(
+                out=i_codes[:, h, :, :].bitcast(I32).rearrange("p i (j b) -> p i j b", b=HALF_SCENES),
+                in_=x1_codes[:, h, :].bitcast(I32).rearrange("p (i b) -> p i b", b=HALF_SCENES)
+                .unsqueeze(2).to_broadcast([P, OBJECTS, OBJECTS, HALF_SCENES]),
+            )
+            nc.vector.tensor_copy(
+                out=i_scales[:, h, :, :].bitcast(I32).rearrange("p i (j w) -> p i j w", w=HALF_SCENES // 4),
+                in_=x1_scales[:, h, :].bitcast(I32).rearrange("p (i w) -> p i w", w=HALF_SCENES // 4)
+                .unsqueeze(2).to_broadcast([P, OBJECTS, OBJECTS, HALF_SCENES // 4]),
+            )
+
+        def quantise_half(h):
+            for c in range(OBJECTS // CHUNK):
+                slices = slice(c * CHUNK, (c + 1) * CHUNK)
+                grouped = stage.tile([P, CHUNK * P * 4], BF16, align_bytes=64)
+                grouped_words = grouped[:].bitcast(F32).rearrange("p (s c u) -> p s c u", s=CHUNK, u=2)
+                for first in range(0, CHUNK, BANK_SLICES):
+                    transpose_bank(
+                        [x2_raw[:, h, c * CHUNK + first + s, :] for s in range(BANK_SLICES)],
+                        grouped_words[:, first : first + BANK_SLICES],
+                    )
+                nc.vector.quantize_mx(
+                    out=ji_codes[:, h, slices, :].rearrange("p q c -> p (q c)").bitcast(FP8X4),
+                    scales=ji_scales[:, h, slices, :].rearrange("p q c -> p (q c)"),
+                    in_=grouped[:],
+                )
+            nc.vector.tensor_copy(
+                out=ij_codes[:, h, :, :].bitcast(I32).rearrange("p i (j b) -> p i j b", b=HALF_SCENES),
+                in_=ji_codes[:, h, :, :].bitcast(I32).rearrange("p j (i b) -> p i j b", b=HALF_SCENES),
+            )
+            nc.vector.tensor_copy(
+                out=ij_scales[:, h, :, :].bitcast(I32).rearrange("p i (j w) -> p i j w", w=HALF_SCENES // 4),
+                in_=ji_scales[:, h, :, :].bitcast(I32).rearrange("p j (i w) -> p i j w", w=HALF_SCENES // 4),
+            )
+
+        def multiply(acc, codes, scales, group, start, stop):
+            nc.tensor.matmul_mx(
+                out=acc[:],
+                lhsT=codes.bitcast(FP8X4),
+                lhsT_scale=scales,
+                rhs=w_words[:, group, :].bitcast(FP4X4),
+                rhs_scale=w_scales[:, group, :],
+                start=start,
+                stop=stop,
+            )
+
+        quantise_half(0)
+
+        bias_acc = psum_acc.tile([P, CHANNELS], F32, tag="acc")
+        nc.tensor.matmul(out=bias_acc[:], lhsT=ones[:], rhs=bias_row[:], start=True, stop=True)
+        nc.scalar.copy(out=bias_all[:], in_=bias_acc[:])
+        for h in range(HALVES):
+            j_acc = psum_acc.tile([P, CHANNELS], F32, tag="acc")
+            multiply(j_acc, x1_codes[:, h, :], x1_scales[:, h, :], W_X1_J, True, True)
+            nc.vector.tensor_tensor(out=j_term[:, h, :], in0=j_acc[:], in1=bias_all[:], op=add)
+
+        quantise_half(1)
+
+        for h in range(HALVES):
+            scenes = slice(h * HALF_SCENES, (h + 1) * HALF_SCENES)
+            for i in range(OBJECTS):
+                acc = psum_acc.tile([P, CHANNELS], F32, tag="acc")
+                multiply(acc, i_codes[:, h, i, :], i_scales[:, h, i, :], W_X1_I, True, False)
+                multiply(acc, ij_codes[:, h, i, :], ij_scales[:, h, i, :], W_X2_IJ, False, False)
+                multiply(acc, ji_codes[:, h, i, :], ji_scales[:, h, i, :], W_X2_JI, False, True)
+                logits = stage.tile([P, CHANNELS], F32)
+                nc.vector.tensor_tensor(out=logits[:], in0=acc[:], in1=j_term[:, h, :], op=add)
+                result = stage.tile([P, CHANNELS], F32)
+                nc.scalar.activation(out=result[:], in_=logits[:], func=sigmoid)
+                nc.sync.dma_start(out=out[scenes, i, :, :].rearrange("b j c -> j b c"), in_=result[:])

@@ -73,12 +73,7 @@ def tile_differentiablelogicmachine_pa_kernel(tc, x1, x2, W2_words, W2_scales, b
         for h in range(HALVES):
             scenes = slice(h * HALF_SCENES, (h + 1) * HALF_SCENES)
             nc.sync.dma_start(out=x1_raw[:, h, :], in_=x1[scenes].rearrange("b i k -> i b k"))
-        for r in range(4):
-            nc.sync.dma_start(
-                out=w_scales[r:P:32, :, :].bitcast(I32),
-                in_=W2_scales[:, r:16:4, :].bitcast(I32).rearrange("g q n -> q g n"),
-            )
-        nc.sync.dma_start(out=bias_row[0:1, :], in_=b2.rearrange("(o c) -> o c", o=1))
+        nc.scalar.dma_start(out=bias_row[0:1, :], in_=b2.rearrange("(o c) -> o c", o=1))
 
         def load_x2_chunk(h, c):
             scenes = slice(h * HALF_SCENES, (h + 1) * HALF_SCENES)
@@ -93,6 +88,11 @@ def tile_differentiablelogicmachine_pa_kernel(tc, x1, x2, W2_words, W2_scales, b
         nc.sync.dma_start(out=w_words[:].bitcast(I32), in_=W2_words.bitcast(I32).rearrange("g p n -> p g n"))
         for c in range(OBJECTS // CHUNK):
             load_x2_chunk(1, c)
+        for r in range(4):
+            nc.sync.dma_start(
+                out=w_scales[r:P:32, :, :].bitcast(I32),
+                in_=W2_scales[:, r:16:4, :].bitcast(I32).rearrange("g q n -> q g n"),
+            )
 
         def transpose_bank(rows_of_slice, grouped_words):
             bank = psum_t.tile([P, 2, BANK_SLICES, P], F32)
@@ -159,6 +159,7 @@ def tile_differentiablelogicmachine_pa_kernel(tc, x1, x2, W2_words, W2_scales, b
             )
 
         quantise_half(0)
+        quantise_half(1)
 
         bias_acc = psum_acc.tile([P, CHANNELS], F32, tag="acc")
         nc.tensor.matmul(out=bias_acc[:], lhsT=ones[:], rhs=bias_row[:], start=True, stop=True)
@@ -167,8 +168,6 @@ def tile_differentiablelogicmachine_pa_kernel(tc, x1, x2, W2_words, W2_scales, b
             j_acc = psum_acc.tile([P, CHANNELS], F32, tag="acc")
             multiply(j_acc, x1_codes[:, h, :], x1_scales[:, h, :], W_X1_J, True, True)
             nc.vector.tensor_tensor(out=j_term[:, h, :], in0=j_acc[:], in1=bias_all[:], op=add)
-
-        quantise_half(1)
 
         for h in range(HALVES):
             scenes = slice(h * HALF_SCENES, (h + 1) * HALF_SCENES)

@@ -38,6 +38,7 @@ def tile_differentiablelogicmachine_pa_kernel(tc, x1, x2, W2_words, W2_scales, b
         ctx.enter_context(tc.manual_schedule())
         keep = ctx.enter_context(tc.tile_pool(name="keep", bufs=1))
         stage = ctx.enter_context(tc.tile_pool(name="stage", bufs=4))
+        results = ctx.enter_context(tc.tile_pool(name="results", bufs=8))
         psum_t = ctx.enter_context(tc.psum_pool(name="psum_t", bufs=4))
         psum_acc = ctx.enter_context(tc.psum_pool(name="psum_acc", bufs=4))
 
@@ -73,7 +74,12 @@ def tile_differentiablelogicmachine_pa_kernel(tc, x1, x2, W2_words, W2_scales, b
         for h in range(HALVES):
             scenes = slice(h * HALF_SCENES, (h + 1) * HALF_SCENES)
             nc.sync.dma_start(out=x1_raw[:, h, :], in_=x1[scenes].rearrange("b i k -> i b k"))
-        nc.scalar.dma_start(out=bias_row[0:1, :], in_=b2.rearrange("(o c) -> o c", o=1))
+        for r in range(4):
+            nc.sync.dma_start(
+                out=w_scales[r:P:32, :, :].bitcast(I32),
+                in_=W2_scales[:, r:16:4, :].bitcast(I32).rearrange("g q n -> q g n"),
+            )
+        nc.sync.dma_start(out=bias_row[0:1, :], in_=b2.rearrange("(o c) -> o c", o=1))
 
         def load_x2_chunk(h, c):
             scenes = slice(h * HALF_SCENES, (h + 1) * HALF_SCENES)
@@ -88,11 +94,6 @@ def tile_differentiablelogicmachine_pa_kernel(tc, x1, x2, W2_words, W2_scales, b
         nc.sync.dma_start(out=w_words[:].bitcast(I32), in_=W2_words.bitcast(I32).rearrange("g p n -> p g n"))
         for c in range(OBJECTS // CHUNK):
             load_x2_chunk(1, c)
-        for r in range(4):
-            nc.sync.dma_start(
-                out=w_scales[r:P:32, :, :].bitcast(I32),
-                in_=W2_scales[:, r:16:4, :].bitcast(I32).rearrange("g q n -> q g n"),
-            )
 
         def transpose_bank(rows_of_slice, grouped_words):
             bank = psum_t.tile([P, 2, BANK_SLICES, P], F32)
@@ -159,7 +160,6 @@ def tile_differentiablelogicmachine_pa_kernel(tc, x1, x2, W2_words, W2_scales, b
             )
 
         quantise_half(0)
-        quantise_half(1)
 
         bias_acc = psum_acc.tile([P, CHANNELS], F32, tag="acc")
         nc.tensor.matmul(out=bias_acc[:], lhsT=ones[:], rhs=bias_row[:], start=True, stop=True)
@@ -168,6 +168,8 @@ def tile_differentiablelogicmachine_pa_kernel(tc, x1, x2, W2_words, W2_scales, b
             j_acc = psum_acc.tile([P, CHANNELS], F32, tag="acc")
             multiply(j_acc, x1_codes[:, h, :], x1_scales[:, h, :], W_X1_J, True, True)
             nc.vector.tensor_tensor(out=j_term[:, h, :], in0=j_acc[:], in1=bias_all[:], op=add)
+
+        quantise_half(1)
 
         for h in range(HALVES):
             scenes = slice(h * HALF_SCENES, (h + 1) * HALF_SCENES)
@@ -178,6 +180,6 @@ def tile_differentiablelogicmachine_pa_kernel(tc, x1, x2, W2_words, W2_scales, b
                 multiply(acc, ji_codes[:, h, i, :], ji_scales[:, h, i, :], W_X2_JI, False, True)
                 logits = stage.tile([P, CHANNELS], F32)
                 nc.vector.tensor_tensor(out=logits[:], in0=acc[:], in1=j_term[:, h, :], op=add)
-                result = stage.tile([P, CHANNELS], F32)
+                result = results.tile([P, CHANNELS], F32)
                 nc.scalar.activation(out=result[:], in_=logits[:], func=sigmoid)
                 nc.sync.dma_start(out=out[scenes, i, :, :].rearrange("b j c -> j b c"), in_=result[:])

@@ -55,6 +55,7 @@ def tile_differentiablelogicmachine_pa_kernel(tc, x1, x2, W2_words, W2_scales, b
         i_codes = keep.tile([P, HALVES, OBJECTS, P], U32, align_bytes=64)
         i_scales = keep.tile([P, HALVES, OBJECTS, P], U8, align_bytes=64)
         identity = keep.tile([P, P], F32)
+        scenes_inner = keep.tile([P, P], F32)
         ones = keep.tile([P, P], BF16)
         bias_row = keep.tile([P, CHANNELS], BF16)
         bias_all = keep.tile([P, CHANNELS], F32)
@@ -70,10 +71,14 @@ def tile_differentiablelogicmachine_pa_kernel(tc, x1, x2, W2_words, W2_scales, b
         nc.vector.memset(warm_in[:], 0.0)
         nc.scalar.activation(out=warm_out[:], in_=warm_in[:], func=sigmoid)
         make_identity(nc, identity[:])
+        nc.vector.tensor_copy(
+            out=scenes_inner[:].rearrange("r (p b) -> r p b", b=HALF_SCENES),
+            in_=identity[:].rearrange("r (b p) -> r p b", p=OBJECTS),
+        )
 
         for h in range(HALVES):
             scenes = slice(h * HALF_SCENES, (h + 1) * HALF_SCENES)
-            nc.sync.dma_start(out=x1_raw[:, h, :], in_=x1[scenes].rearrange("b i k -> i b k"))
+            nc.sync.dma_start(out=x1_raw[:, h, :], in_=x1[scenes].rearrange("b i k -> (b i) k"))
         for r in range(4):
             nc.sync.dma_start(
                 out=w_scales[r:P:32, :, :].bitcast(I32),
@@ -86,7 +91,7 @@ def tile_differentiablelogicmachine_pa_kernel(tc, x1, x2, W2_words, W2_scales, b
             slices = slice(c * CHUNK, (c + 1) * CHUNK)
             nc.sync.dma_start(
                 out=x2_raw[:, h, slices, :].rearrange("p q k -> p (q k)"),
-                in_=x2[scenes, :, slices, :].rearrange("b p q k -> p b (q k)"),
+                in_=x2[scenes, :, slices, :].rearrange("b p q k -> (b p) (q k)"),
             )
 
         for c in range(OBJECTS // CHUNK):
@@ -99,7 +104,7 @@ def tile_differentiablelogicmachine_pa_kernel(tc, x1, x2, W2_words, W2_scales, b
             bank = psum_t.tile([P, 2, BANK_SLICES, P], F32)
             for s in range(BANK_SLICES):
                 for u in range(2):
-                    nc.tensor.transpose(bank[:, u, s, :], rows_of_slice[s].bitcast(F32)[:, u:WORDS:2], identity[:])
+                    nc.tensor.transpose(bank[:, u, s, :], rows_of_slice[s].bitcast(F32)[:, u:WORDS:2], scenes_inner[:])
             nc.scalar.copy(out=grouped_words, in_=bank[:].rearrange("p u s c -> p s c u"))
 
         x1_grouped = keep.tile([P, HALVES * P * 4], BF16, align_bytes=64)

@@ -94,11 +94,10 @@ def tile_differentiablelogicmachine_pa_kernel(tc, x1, x2, W2_words, W2_scales, b
                 in_=x2[scenes, :, slices, :].rearrange("b p q k -> (b p) (q k)"),
             )
 
-        for c in range(OBJECTS // CHUNK):
-            load_x2_chunk(0, c)
+        for h in range(HALVES):
+            for c in range(OBJECTS // CHUNK):
+                load_x2_chunk(h, c)
         nc.sync.dma_start(out=w_words[:].bitcast(I32), in_=W2_words.bitcast(I32).rearrange("g p n -> p g n"))
-        for c in range(OBJECTS // CHUNK):
-            load_x2_chunk(1, c)
 
         def transpose_bank(rows_of_slice, grouped_words):
             bank = psum_t.tile([P, 2, BANK_SLICES, P], F32)
@@ -165,6 +164,7 @@ def tile_differentiablelogicmachine_pa_kernel(tc, x1, x2, W2_words, W2_scales, b
             )
 
         quantise_half(0)
+        quantise_half(1)
 
         bias_acc = psum_acc.tile([P, CHANNELS], F32, tag="acc")
         nc.tensor.matmul(out=bias_acc[:], lhsT=ones[:], rhs=bias_row[:], start=True, stop=True)
@@ -173,8 +173,6 @@ def tile_differentiablelogicmachine_pa_kernel(tc, x1, x2, W2_words, W2_scales, b
             j_acc = psum_acc.tile([P, CHANNELS], F32, tag="acc")
             multiply(j_acc, x1_codes[:, h, :], x1_scales[:, h, :], W_X1_J, True, True)
             nc.vector.tensor_tensor(out=j_term[:, h, :], in0=j_acc[:], in1=bias_all[:], op=add)
-
-        quantise_half(1)
 
         for h in range(HALVES):
             scenes = slice(h * HALF_SCENES, (h + 1) * HALF_SCENES)

@@ -35,7 +35,6 @@ def tile_differentiablelogicmachine_pa_kernel(tc, x1, x2, W2_words, W2_scales, b
     sigmoid = mybir.ActivationFunctionType.Sigmoid
 
     with ExitStack() as ctx:
-        ctx.enter_context(tc.manual_schedule())
         keep = ctx.enter_context(tc.tile_pool(name="keep", bufs=1))
         stage = ctx.enter_context(tc.tile_pool(name="stage", bufs=4))
         results = ctx.enter_context(tc.tile_pool(name="results", bufs=8))

@@ -78,12 +78,6 @@ def tile_differentiablelogicmachine_pa_kernel(tc, x1, x2, W2_words, W2_scales, b
         for h in range(HALVES):
             scenes = slice(h * HALF_SCENES, (h + 1) * HALF_SCENES)
             nc.sync.dma_start(out=x1_raw[:, h, :], in_=x1[scenes].rearrange("b i k -> (b i) k"))
-        for r in range(4):
-            nc.sync.dma_start(
-                out=w_scales[r:P:32, :, :].bitcast(I32),
-                in_=W2_scales[:, r:16:4, :].bitcast(I32).rearrange("g q n -> q g n"),
-            )
-        nc.sync.dma_start(out=bias_row[0:1, :], in_=b2.rearrange("(o c) -> o c", o=1))
 
         def load_x2_chunk(h, c):
             scenes = slice(h * HALF_SCENES, (h + 1) * HALF_SCENES)
@@ -97,6 +91,12 @@ def tile_differentiablelogicmachine_pa_kernel(tc, x1, x2, W2_words, W2_scales, b
             for c in range(OBJECTS // CHUNK):
                 load_x2_chunk(h, c)
         nc.sync.dma_start(out=w_words[:].bitcast(I32), in_=W2_words.bitcast(I32).rearrange("g p n -> p g n"))
+        for r in range(4):
+            nc.sync.dma_start(
+                out=w_scales[r:P:32, :, :].bitcast(I32),
+                in_=W2_scales[:, r:16:4, :].bitcast(I32).rearrange("g q n -> q g n"),
+            )
+        nc.sync.dma_start(out=bias_row[0:1, :], in_=b2.rearrange("(o c) -> o c", o=1))
 
         def transpose_bank(rows_of_slice, grouped_words):
             bank = psum_t.tile([P, 2, BANK_SLICES, P], F32)
@@ -115,7 +115,7 @@ def tile_differentiablelogicmachine_pa_kernel(tc, x1, x2, W2_words, W2_scales, b
             scales=x1_scales[:].rearrange("p h c -> p (h c)"),
             in_=x1_grouped[:],
         )
-        for h in range(HALVES):
+        def repeat_x1(h):
             nc.vector.tensor_copy(
                 out=i_codes[:, h, :, :].bitcast(I32).rearrange("p i (j b) -> p i j b", b=HALF_SCENES),
                 in_=x1_codes[:, h, :].bitcast(I32).rearrange("p (i b) -> p i b", b=HALF_SCENES)
@@ -126,6 +126,8 @@ def tile_differentiablelogicmachine_pa_kernel(tc, x1, x2, W2_words, W2_scales, b
                 in_=x1_scales[:, h, :].bitcast(I32).rearrange("p (i w) -> p i w", w=HALF_SCENES // 4)
                 .unsqueeze(2).to_broadcast([P, OBJECTS, OBJECTS, HALF_SCENES // 4]),
             )
+
+        repeat_x1(0)
 
         def quantise_half(h):
             for c in range(OBJECTS // CHUNK):
@@ -142,6 +144,7 @@ def tile_differentiablelogicmachine_pa_kernel(tc, x1, x2, W2_words, W2_scales, b
                     scales=ji_scales[:, h, slices, :].rearrange("p q c -> p (q c)"),
                     in_=grouped[:],
                 )
+        def exchange_half(h):
             nc.vector.tensor_copy(
                 out=ij_codes[:, h, :, :].bitcast(I32).rearrange("p i (j b) -> p i j b", b=HALF_SCENES),
                 in_=ji_codes[:, h, :, :].bitcast(I32).rearrange("p j (i b) -> p i j b", b=HALF_SCENES),
@@ -163,6 +166,7 @@ def tile_differentiablelogicmachine_pa_kernel(tc, x1, x2, W2_words, W2_scales, b
             )
 
         quantise_half(0)
+        exchange_half(0)
         quantise_half(1)
 
         bias_acc = psum_acc.tile([P, CHANNELS], F32, tag="acc")
@@ -185,3 +189,7 @@ def tile_differentiablelogicmachine_pa_kernel(tc, x1, x2, W2_words, W2_scales, b
                 result = results.tile([P, CHANNELS], F32)
                 nc.scalar.activation(out=result[:], in_=logits[:], func=sigmoid)
                 nc.sync.dma_start(out=out[scenes, i, :, :].rearrange("b j c -> j b c"), in_=result[:])
+                if h == 0 and i == 5:
+                    repeat_x1(1)
+                if h == 0 and i == 9:
+                    exchange_half(1)

@@ -43,16 +43,16 @@ def tile_differentiablelogicmachine_pa_kernel(tc, x1, x2, W2_words, W2_scales, b
 
         x1_raw = keep.tile([P, HALVES, CHANNELS], BF16)
         x2_raw = keep.tile([P, HALVES, OBJECTS, CHANNELS], BF16)
-        w_words = keep.tile([P, 4, 2 * CHANNELS], U8, align_bytes=64)
-        w_scales = keep.tile([P, 4, CHANNELS], U8, align_bytes=64)
-        x1_codes = keep.tile([P, HALVES, P], U32, align_bytes=64)
-        x1_scales = keep.tile([P, HALVES, P], U8, align_bytes=64)
-        ji_codes = keep.tile([P, HALVES, OBJECTS, P], U32, align_bytes=64)
-        ji_scales = keep.tile([P, HALVES, OBJECTS, P], U8, align_bytes=64)
-        ij_codes = keep.tile([P, HALVES, OBJECTS, P], U32, align_bytes=64)
-        ij_scales = keep.tile([P, HALVES, OBJECTS, P], U8, align_bytes=64)
-        i_codes = keep.tile([P, HALVES, OBJECTS, P], U32, align_bytes=64)
-        i_scales = keep.tile([P, HALVES, OBJECTS, P], U8, align_bytes=64)
+        w_words = keep.tile([P, 4, 2 * CHANNELS], U8, align_bytes=256)
+        w_scales = keep.tile([P, 4, CHANNELS], U8, align_bytes=256)
+        x1_codes = keep.tile([P, HALVES, P], U32, align_bytes=256)
+        x1_scales = keep.tile([P, HALVES, P], U8, align_bytes=256)
+        ji_codes = keep.tile([P, HALVES, OBJECTS, P], U32, align_bytes=256)
+        ji_scales = keep.tile([P, HALVES, OBJECTS, P], U8, align_bytes=256)
+        ij_codes = keep.tile([P, HALVES, OBJECTS, P], U32, align_bytes=256)
+        ij_scales = keep.tile([P, HALVES, OBJECTS, P], U8, align_bytes=256)
+        i_codes = keep.tile([P, HALVES, OBJECTS, P], U32, align_bytes=256)
+        i_scales = keep.tile([P, HALVES, OBJECTS, P], U8, align_bytes=256)
         identity = keep.tile([P, P], F32)
         scenes_inner = keep.tile([P, P], F32)
         ones = keep.tile([P, P], BF16)
@@ -105,7 +105,7 @@ def tile_differentiablelogicmachine_pa_kernel(tc, x1, x2, W2_words, W2_scales, b
                     nc.tensor.transpose(bank[:, u, s, :], rows_of_slice[s].bitcast(F32)[:, u:WORDS:2], scenes_inner[:])
             nc.scalar.copy(out=grouped_words, in_=bank[:].rearrange("p u s c -> p s c u"))
 
-        x1_grouped = keep.tile([P, HALVES * P * 4], BF16, align_bytes=64)
+        x1_grouped = keep.tile([P, HALVES * P * 4], BF16, align_bytes=256)
         transpose_bank(
             [x1_raw[:, h, :] for h in range(HALVES)],
             x1_grouped[:].bitcast(F32).rearrange("p (s c u) -> p s c u", s=BANK_SLICES, u=2),
@@ -132,7 +132,7 @@ def tile_differentiablelogicmachine_pa_kernel(tc, x1, x2, W2_words, W2_scales, b
         def quantise_half(h):
             for c in range(OBJECTS // CHUNK):
                 slices = slice(c * CHUNK, (c + 1) * CHUNK)
-                grouped = stage.tile([P, CHUNK * P * 4], BF16, align_bytes=64)
+                grouped = stage.tile([P, CHUNK * P * 4], BF16, align_bytes=256)
                 grouped_words = grouped[:].bitcast(F32).rearrange("p (s c u) -> p s c u", s=CHUNK, u=2)
                 for first in range(0, CHUNK, BANK_SLICES):
                     transpose_bank(

from contextlib import ExitStack

import concourse.mybir as mybir
from concourse.masks import make_identity

F32 = mybir.dt.float32
BF16 = mybir.dt.bfloat16
I32 = mybir.dt.int32
U32 = mybir.dt.uint32
U8 = mybir.dt.uint8
FP8X4 = mybir.dt.float8_e4m3fn_x4
FP4X4 = mybir.dt.float4_e2m1fn_x4

P = 128
SCENES = 16
OBJECTS = 16
CHANNELS = 512
HALVES = 2
HALF_SCENES = SCENES // HALVES
WORDS = CHANNELS // 2
CHUNK = 4
BANK_SLICES = 2

W_X1_I = 0
W_X2_IJ = 1
W_X1_J = 2
W_X2_JI = 3

FLOPS = 2 * SCENES * OBJECTS * OBJECTS * 4 * CHANNELS * CHANNELS


def tile_differentiablelogicmachine_pa_kernel(tc, x1, x2, W2_words, W2_scales, b2, out):
    nc = tc.nc
    add = mybir.AluOpType.add
    sigmoid = mybir.ActivationFunctionType.Sigmoid

    with ExitStack() as ctx:
        keep = ctx.enter_context(tc.tile_pool(name="keep", bufs=1))
        stage = ctx.enter_context(tc.tile_pool(name="stage", bufs=4))
        results = ctx.enter_context(tc.tile_pool(name="results", bufs=8))
        psum_t = ctx.enter_context(tc.psum_pool(name="psum_t", bufs=4))
        psum_acc = ctx.enter_context(tc.psum_pool(name="psum_acc", bufs=4))

        x1_raw = keep.tile([P, HALVES, CHANNELS], BF16)
        x2_raw = keep.tile([P, HALVES, OBJECTS, CHANNELS], BF16)
        w_words = keep.tile([P, 4, 2 * CHANNELS], U8, align_bytes=256)
        w_scales = keep.tile([P, 4, CHANNELS], U8, align_bytes=256)
        x1_codes = keep.tile([P, HALVES, P], U32, align_bytes=256)
        x1_scales = keep.tile([P, HALVES, P], U8, align_bytes=256)
        ji_codes = keep.tile([P, HALVES, OBJECTS, P], U32, align_bytes=256)
        ji_scales = keep.tile([P, HALVES, OBJECTS, P], U8, align_bytes=256)
        ij_codes = keep.tile([P, HALVES, OBJECTS, P], U32, align_bytes=256)
        ij_scales = keep.tile([P, HALVES, OBJECTS, P], U8, align_bytes=256)
        i_codes = keep.tile([P, HALVES, OBJECTS, P], U32, align_bytes=256)
        i_scales = keep.tile([P, HALVES, OBJECTS, P], U8, align_bytes=256)
        identity = keep.tile([P, P], F32)
        scenes_inner = keep.tile([P, P], F32)
        ones = keep.tile([P, P], BF16)
        bias_row = keep.tile([P, CHANNELS], BF16)
        bias_all = keep.tile([P, CHANNELS], F32)
        j_term = keep.tile([P, HALVES, CHANNELS], F32)
        warm_in = keep.tile([P, 1], F32)
        warm_out = keep.tile([P, 1], F32)

        nc.vector.memset(w_scales[:].bitcast(I32), 0)
        nc.vector.memset(x1_scales[:].bitcast(I32), 0)
        nc.vector.memset(ji_scales[:].bitcast(I32), 0)
        nc.vector.memset(bias_row[:], 0.0)
        nc.vector.memset(ones[:], 1.0)
        nc.vector.memset(warm_in[:], 0.0)
        nc.scalar.activation(out=warm_out[:], in_=warm_in[:], func=sigmoid)
        make_identity(nc, identity[:])
        nc.vector.tensor_copy(
            out=scenes_inner[:].rearrange("r (p b) -> r p b", b=HALF_SCENES),
            in_=identity[:].rearrange("r (b p) -> r p b", p=OBJECTS),
        )

        for h in range(HALVES):
            scenes = slice(h * HALF_SCENES, (h + 1) * HALF_SCENES)
            nc.sync.dma_start(out=x1_raw[:, h, :], in_=x1[scenes].rearrange("b i k -> (b i) k"))

        def load_x2_chunk(h, c):
            scenes = slice(h * HALF_SCENES, (h + 1) * HALF_SCENES)
            slices = slice(c * CHUNK, (c + 1) * CHUNK)
            nc.sync.dma_start(
                out=x2_raw[:, h, slices, :].rearrange("p q k -> p (q k)"),
                in_=x2[scenes, :, slices, :].rearrange("b p q k -> (b p) (q k)"),
            )

        for h in range(HALVES):
            for c in range(OBJECTS // CHUNK):
                load_x2_chunk(h, c)
        nc.sync.dma_start(out=w_words[:].bitcast(I32), in_=W2_words.bitcast(I32).rearrange("g p n -> p g n"))
        for r in range(4):
            nc.sync.dma_start(
                out=w_scales[r:P:32, :, :].bitcast(I32),
                in_=W2_scales[:, r:16:4, :].bitcast(I32).rearrange("g q n -> q g n"),
            )
        nc.sync.dma_start(out=bias_row[0:1, :], in_=b2.rearrange("(o c) -> o c", o=1))

        def transpose_bank(rows_of_slice, grouped_words):
            bank = psum_t.tile([P, 2, BANK_SLICES, P], F32)
            for s in range(BANK_SLICES):
                for u in range(2):
                    nc.tensor.transpose(bank[:, u, s, :], rows_of_slice[s].bitcast(F32)[:, u:WORDS:2], scenes_inner[:])
            nc.scalar.copy(out=grouped_words, in_=bank[:].rearrange("p u s c -> p s c u"))

        x1_grouped = keep.tile([P, HALVES * P * 4], BF16, align_bytes=256)
        transpose_bank(
            [x1_raw[:, h, :] for h in range(HALVES)],
            x1_grouped[:].bitcast(F32).rearrange("p (s c u) -> p s c u", s=BANK_SLICES, u=2),
        )
        nc.vector.quantize_mx(
            out=x1_codes[:].rearrange("p h c -> p (h c)").bitcast(FP8X4),
            scales=x1_scales[:].rearrange("p h c -> p (h c)"),
            in_=x1_grouped[:],
        )
        def repeat_x1(h):
            nc.vector.tensor_copy(
                out=i_codes[:, h, :, :].bitcast(I32).rearrange("p i (j b) -> p i j b", b=HALF_SCENES),
                in_=x1_codes[:, h, :].bitcast(I32).rearrange("p (i b) -> p i b", b=HALF_SCENES)
                .unsqueeze(2).to_broadcast([P, OBJECTS, OBJECTS, HALF_SCENES]),
            )
            nc.vector.tensor_copy(
                out=i_scales[:, h, :, :].bitcast(I32).rearrange("p i (j w) -> p i j w", w=HALF_SCENES // 4),
                in_=x1_scales[:, h, :].bitcast(I32).rearrange("p (i w) -> p i w", w=HALF_SCENES // 4)
                .unsqueeze(2).to_broadcast([P, OBJECTS, OBJECTS, HALF_SCENES // 4]),
            )

        repeat_x1(0)

        def quantise_half(h):
            for c in range(OBJECTS // CHUNK):
                slices = slice(c * CHUNK, (c + 1) * CHUNK)
                grouped = stage.tile([P, CHUNK * P * 4], BF16, align_bytes=256)
                grouped_words = grouped[:].bitcast(F32).rearrange("p (s c u) -> p s c u", s=CHUNK, u=2)
                for first in range(0, CHUNK, BANK_SLICES):
                    transpose_bank(
                        [x2_raw[:, h, c * CHUNK + first + s, :] for s in range(BANK_SLICES)],
                        grouped_words[:, first : first + BANK_SLICES],
                    )
                nc.vector.quantize_mx(
                    out=ji_codes[:, h, slices, :].rearrange("p q c -> p (q c)").bitcast(FP8X4),
                    scales=ji_scales[:, h, slices, :].rearrange("p q c -> p (q c)"),
                    in_=grouped[:],
                )
        def exchange_half(h):
            nc.vector.tensor_copy(
                out=ij_codes[:, h, :, :].bitcast(I32).rearrange("p i (j b) -> p i j b", b=HALF_SCENES),
                in_=ji_codes[:, h, :, :].bitcast(I32).rearrange("p j (i b) -> p i j b", b=HALF_SCENES),
            )
            nc.vector.tensor_copy(
                out=ij_scales[:, h, :, :].bitcast(I32).rearrange("p i (j w) -> p i j w", w=HALF_SCENES // 4),
                in_=ji_scales[:, h, :, :].bitcast(I32).rearrange("p j (i w) -> p i j w", w=HALF_SCENES // 4),
            )

        def multiply(acc, codes, scales, group, start, stop):
            nc.tensor.matmul_mx(
                out=acc[:],
                lhsT=codes.bitcast(FP8X4),
                lhsT_scale=scales,
                rhs=w_words[:, group, :].bitcast(FP4X4),
                rhs_scale=w_scales[:, group, :],
                start=start,
                stop=stop,
            )

        quantise_half(0)
        exchange_half(0)
        quantise_half(1)

        bias_acc = psum_acc.tile([P, CHANNELS], F32, tag="acc")
        nc.tensor.matmul(out=bias_acc[:], lhsT=ones[:], rhs=bias_row[:], start=True, stop=True)
        nc.scalar.copy(out=bias_all[:], in_=bias_acc[:])
        for h in range(HALVES):
            j_acc = psum_acc.tile([P, CHANNELS], F32, tag="acc")
            multiply(j_acc, x1_codes[:, h, :], x1_scales[:, h, :], W_X1_J, True, True)
            nc.vector.tensor_tensor(out=j_term[:, h, :], in0=j_acc[:], in1=bias_all[:], op=add)

        for h in range(HALVES):
            scenes = slice(h * HALF_SCENES, (h + 1) * HALF_SCENES)
            for i in range(OBJECTS):
                acc = psum_acc.tile([P, CHANNELS], F32, tag="acc")
                multiply(acc, i_codes[:, h, i, :], i_scales[:, h, i, :], W_X1_I, True, False)
                multiply(acc, ij_codes[:, h, i, :], ij_scales[:, h, i, :], W_X2_IJ, False, False)
                multiply(acc, ji_codes[:, h, i, :], ji_scales[:, h, i, :], W_X2_JI, False, True)
                logits = stage.tile([P, CHANNELS], F32)
                nc.vector.tensor_tensor(out=logits[:], in0=acc[:], in1=j_term[:, h, :], op=add)
                result = results.tile([P, CHANNELS], F32)
                nc.scalar.activation(out=result[:], in_=logits[:], func=sigmoid)
                nc.sync.dma_start(out=out[scenes, i, :, :].rearrange("b j c -> j b c"), in_=result[:])
                if h == 0 and i == 5:
                    repeat_x1(1)
                if h == 0 and i == 9:
                    exchange_half(1)
